import numpy as np
import ml_dtypes


def mxq(x, axis, fmt="e4m3"):
    dtype, down = {"e4m3": (ml_dtypes.float8_e4m3fn, 7), "e5m2": (ml_dtypes.float8_e5m2, 14)}[fmt]
    v = np.moveaxis(np.asarray(x, np.float32).astype(ml_dtypes.bfloat16).astype(np.float64), axis, -1)
    blocks = v.reshape(v.shape[:-1] + (-1, 32))
    amax = np.abs(blocks).max(-1, keepdims=True)
    byte = np.maximum(np.where(amax > 0, np.frexp(amax)[1] - 1 + 127, 0) - down, 1)
    scale = np.exp2(byte - 127.0)
    codes = (blocks / scale).astype(np.float32).astype(dtype).astype(np.float64)
    return np.moveaxis((codes * scale).reshape(v.shape), -1, axis)


WIDE = False


def mx_kscale(k):
    if not WIDE:
        return np.ones(k)
    levels = np.array([10, -10, 5, -5, 0])
    if k % 512:
        return np.exp2(np.random.permutation(np.resize(levels, k // 32))).repeat(32)
    a = np.empty((k // 512, 16))
    for p in range(k // 512):
        a[p, :8] = np.random.permutation(np.resize(levels, 8))
        for g in range(8):
            far = levels[np.abs(levels - a[p, g]) >= 10]
            a[p, g + 8] = far[np.random.randint(len(far))]
    return np.exp2(a.ravel()).repeat(32)


BF16 = ml_dtypes.bfloat16


def bf(x):
    return np.asarray(x, np.float32).astype(BF16)


def f64(x):
    return np.asarray(x).astype(np.float64)


NB, D, CO, CV, R = 16, 256, 128, 512, 512


def setup_inputs():
    s, t = mx_kscale(CV), mx_kscale(R)
    return {"x1": bf(np.random.standard_normal((NB, D, CO))),
            "A": bf(np.random.standard_normal((D, R)) / np.sqrt(D) * t),
            "t2": bf(np.random.standard_normal((NB, R, CV)) * s),
            "w": bf(np.random.standard_normal((NB, CO, CV)) / np.sqrt(CV) / s),
            "C": bf(np.random.standard_normal((D, R)) / np.sqrt(R) / t)}


def reference(x1, A, t2, w, C):
    t1 = f64(A).T @ f64(x1)
    t3 = f64(bf(mxq(f64(t2), 2, "e4m3") @ mxq(f64(w).transpose(0, 2, 1), 1, "e4m3")))
    h = t1 * t3
    return mxq(f64(C), 1, "e4m3") @ mxq(h, 1, "e4m3")

@@ -1,0 +1,215 @@
+from contextlib import ExitStack
+
+import concourse.mybir as mybir
+from concourse.masks import make_identity
+
+NB, D, CO, CV, R = 16, 256, 128, 512, 512
+FLOPS = 2 * NB * CO * (R * D + R * CV + D * R)
+
+F32 = mybir.dt.float32
+BF16 = mybir.dt.bfloat16
+U32 = mybir.dt.uint32
+U8 = mybir.dt.uint8
+FP8X4 = mybir.dt.float8_e4m3fn_x4
+T3_DT = BF16
+
+P = 128
+NPAIR = NB // 2
+C_TICK = 2
+GROUPS = [(b, 2) for b in range(0, NB - 2, 2)] + [(NB - 2, 1), (NB - 1, 1)]
+
+
+def tile_cptensorproduct_pa_kernel(tc, x1, A, t2, w, C, out):
+    nc = tc.nc
+    with ExitStack() as ctx:
+        keep = ctx.enter_context(tc.tile_pool(name="keep", bufs=1))
+        work = ctx.enter_context(tc.tile_pool(name="work", bufs=3))
+        psum = ctx.enter_context(tc.psum_pool(name="psum", bufs=1))
+        ctx.enter_context(tc.manual_schedule())
+
+        t2_sb = [keep.tile([P, 4 * CV], BF16, name="t2_sb%d" % b, tag="t2_sb%d" % b) for b in range(NB)]
+        w_sb = [keep.tile([P, 2, CV], BF16, name="w_sb%d" % k, tag="w_sb%d" % k) for k in range(NPAIR)]
+        x1_sb = [keep.tile([P, 4, 2 * CO], BF16, name="x1_sb%d" % g, tag="x1_sb%d" % g) for g in range(NB // 4)]
+        o_sb = [keep.tile([P, n, 2, CO], F32, name="o_sb%d" % b, tag="o_sb%d" % b) for b, n in GROUPS]
+        a_raw = keep.tile([P, 2 * R], BF16, name="a_raw", tag="a_raw")
+        c_raw = keep.tile([P, 2 * R], BF16, name="c_raw", tag="c_raw")
+
+        def load_w(k):
+            nc.sync.dma_start(out=w_sb[k][:], in_=w[2 * k : 2 * k + 2].rearrange("b c k -> c b k"))
+
+        load_w(0)
+        for b in range(NB):
+            nc.sync.dma_start(out=t2_sb[b][:], in_=t2[b].rearrange("(m t) k -> m (t k)", t=4))
+            if b % 2 == 1 and (b + 1) // 2 < NPAIR:
+                load_w((b + 1) // 2)
+            if b == 1:
+                nc.sync.dma_start(out=a_raw[:], in_=A.rearrange("(p e) r -> p (e r)", e=2))
+            if b % 4 == 1:
+                g = b // 4
+                nc.sync.dma_start(
+                    out=x1_sb[g][:], in_=x1[4 * g : 4 * g + 4].rearrange("b (p e) c -> p b (e c)", e=2)
+                )
+            if b == C_TICK + 2:
+                nc.sync.dma_start(out=c_raw[:], in_=C.rearrange("(p e) r -> p (e r)", e=2))
+
+        ident = keep.tile([P, P], F32, name="ident", tag="ident")
+        make_identity(nc, ident[:])
+        a_perm = keep.tile([P, 2, 4, P], BF16, name="a_perm", tag="a_perm")
+        c_grouped = keep.tile([P, 4 * D], BF16, name="c_grouped", tag="c_grouped", align_bytes=64)
+        c_codes = keep.tile([P, D], U32, name="c_codes", tag="c_codes", align_bytes=64)
+        c_scales = keep.tile([P, D], U8, name="c_scales", tag="c_scales", align_bytes=64)
+
+        def half(words, h, grouped):
+            bank = psum.tile([P, 2, 2, P], F32, name="tp", tag="tp", bufs=5)
+            trs = []
+            for s in (0, 1):
+                for u in (0, 1):
+                    lo = 256 * (2 * h + s)
+                    trs.append((bank[:, s, u, :], words[:, lo + u : lo + 256 : 2]))
+            dst = grouped[:].bitcast(F32)[:, 512 * h : 512 * (h + 1)].rearrange("p (s m u) -> p s m u", s=2, u=2)
+            return trs, (dst, bank[:].rearrange("p s u m -> p s m u"))
+
+        def quantize(grouped, codes, scales):
+            nc.vector.quantize_mx(out=codes[:].bitcast(FP8X4), scales=scales[:], in_=grouped[:])
+
+        def t1_matmuls(b, slots):
+            for t in slots:
+                for e in (0, 1):
+                    nc.tensor.matmul(
+                        t1_ps[b][:, t, :],
+                        lhsT=a_perm[:, e, t, :],
+                        rhs=x1_sb[b // 4][:, b % 4, CO * e : CO * (e + 1)],
+                        start=(e == 0),
+                        stop=(e == 1),
+                    )
+
+        t2_q = {}
+        w_q = {}
+        h_grouped = {}
+        h_q = {}
+        t1_ps = {}
+        t3_sb = {}
+        w_rest = []
+        quants = []
+
+        for i in range(-3, NB + 3):
+            j = i + 2
+            t3 = None
+            if 0 <= i < NB:
+                t1_ps[i] = psum.tile([P, 4, CO], F32, name="t1", tag="t1", bufs=2)
+                t1_matmuls(i, (0, 1))
+                t3 = psum.tile([P, 4, CO], T3_DT, name="t3", tag="t3", bufs=1)
+                tcd, tsc = t2_q[i]
+                wc, ws = w_q[i // 2]
+                cols = slice(CO * (i % 2), CO * (i % 2 + 1))
+                for t in range(4):
+                    rows = slice(P * t, P * (t + 1))
+                    nc.tensor.matmul_mx(
+                        out=t3[:, t, :],
+                        lhsT=tcd[:, rows].bitcast(FP8X4),
+                        lhsT_scale=tsc[:, rows],
+                        rhs=wc[:, cols].bitcast(FP8X4),
+                        rhs_scale=ws[:, cols],
+                        start=True,
+                        stop=True,
+                    )
+            outs = []
+            for k, (b0, n) in enumerate(GROUPS):
+                if b0 + n + 2 == i:
+                    o_ps = psum.tile([P, 2, n * CO], F32, name="o_ps", tag="tp", bufs=5)
+                    hc, hs = h_q[k]
+                    for e in (0, 1):
+                        rows = slice(P * e, P * (e + 1))
+                        nc.tensor.matmul_mx(
+                            out=o_ps[:, e, :],
+                            lhsT=c_codes[:, rows].bitcast(FP8X4),
+                            lhsT_scale=c_scales[:, rows],
+                            rhs=hc[:].bitcast(FP8X4),
+                            rhs_scale=hs[:],
+                            start=True,
+                            stop=True,
+                        )
+                    outs.append((k, b0, n, o_ps))
+            if 0 <= i < NB:
+                t1_matmuls(i, (2, 3))
+
+            trs = []
+            copies = []
+            done = []
+            for t, c, q in w_rest:
+                trs += t
+                copies.append(c)
+                done.append(q)
+            w_rest = []
+            if 0 <= j < NB:
+                tg = work.tile([P, 4 * R], BF16, name="tg", tag="tg", align_bytes=64)
+                tcd = work.tile([P, R], U32, name="tcd", tag="tcd", align_bytes=64)
+                tsc = work.tile([P, R], U8, name="tsc", tag="tsc", align_bytes=64)
+                for h in (0, 1):
+                    t, c = half(t2_sb[j][:].bitcast(F32), h, tg)
+                    trs += t
+                    copies.append(c)
+                done.append((tg, tcd, tsc))
+                t2_q[j] = (tcd, tsc)
+            if i % 2 == 1 and (i + 3) // 2 < NPAIR:
+                k = (i + 3) // 2
+                wg = work.tile([P, 4 * 2 * CO], BF16, name="wg", tag="wg", align_bytes=64)
+                wc = work.tile([P, 2 * CO], U32, name="wc", tag="wc", align_bytes=64)
+                ws = work.tile([P, 2 * CO], U8, name="ws", tag="ws", align_bytes=64)
+                t, c = half(w_sb[k][:].rearrange("p b k -> p (b k)").bitcast(F32), 0, wg)
+                w_q[k] = (wc, ws)
+                if k == 0:
+                    trs += t
+                    copies.append(c)
+                    done.append((wg, wc, ws))
+                else:
+                    trs += t[:2]
+                    w_rest.append((t[2:], c, (wg, wc, ws)))
+            if i == C_TICK:
+                t, c = half(c_raw[:].bitcast(F32), 0, c_grouped)
+                trs += t
+                copies.append(c)
+                done.append((c_grouped, c_codes, c_scales))
+            for o, s in trs:
+                nc.tensor.transpose(o, s, ident[:])
+
+            if t3 is not None:
+                t3_sb[i] = work.tile([P, 4, CO], T3_DT, name="t3c", tag="t3c")
+                nc.scalar.copy(out=t3_sb[i][:], in_=t3[:])
+            for dst, src in copies:
+                nc.scalar.copy(out=dst, in_=src)
+
+            for k, (b0, n) in enumerate(GROUPS):
+                if b0 == i - 1:
+                    h_grouped[k] = work.tile([P, n * CO * 4], BF16, name="hg", tag="hg", align_bytes=64)
+                if b0 <= i - 1 < b0 + n:
+                    lo = 4 * CO * (i - 1 - b0)
+                    nc.vector.tensor_tensor(
+                        out=h_grouped[k][:, lo : lo + 4 * CO].rearrange("p (c t) -> p c t", t=4),
+                        in0=t1_ps[i - 1][:].rearrange("p t c -> p c t"),
+                        in1=t3_sb[i - 1][:].rearrange("p t c -> p c t"),
+                        op=mybir.AluOpType.mult,
+                    )
+            for grouped, codes, scales in quants:
+                quantize(grouped, codes, scales)
+            quants = done
+            if i == -1:
+                nc.vector.tensor_copy(out=a_perm[:], in_=a_raw[:].rearrange("p (e m t) -> p e t m", e=2, t=4))
+            for k, (b0, n) in enumerate(GROUPS):
+                if b0 + n + 1 == i:
+                    hc = work.tile([P, n * CO], U32, name="hc", tag="hc", align_bytes=64)
+                    hs = work.tile([P, n * CO], U8, name="hs", tag="hs", align_bytes=64)
+                    quantize(h_grouped[k], hc, hs)
+                    h_q[k] = (hc, hs)
+
+            for k, b0, n, o_ps in outs:
+                dst = o_sb[k][:].rearrange("p b e c -> p e b c")
+                src = o_ps[:].rearrange("p e (b c) -> p e b c", b=n)
+                if i < NB:
+                    nc.vector.tensor_copy(out=dst, in_=src)
+                else:
+                    nc.scalar.copy(out=dst, in_=src)
+                nc.sync.dma_start(
+                    out=out[b0 : b0 + n].rearrange("b (p e) c -> p b (e c)", e=2),
+                    in_=o_sb[k][:].rearrange("p b e c -> p b (e c)"),
+                )

@@ -15,7 +15,8 @@ T3_DT = BF16
 
 P = 128
 NPAIR = NB // 2
-C_TICK = 2
+C_TICK = 4
+SORT_FROM = 3
 GROUPS = [(b, 2) for b in range(0, NB - 2, 2)] + [(NB - 2, 1), (NB - 1, 1)]
 
 
@@ -59,13 +60,16 @@ def tile_cptensorproduct_pa_kernel(tc, x1, A, t2, w, C, out):
         c_codes = keep.tile([P, D], U32, name="c_codes", tag="c_codes", align_bytes=64)
         c_scales = keep.tile([P, D], U8, name="c_scales", tag="c_scales", align_bytes=64)
 
-        def half(words, h, grouped):
+        def half(words, h, grouped, ordered=None):
             bank = psum.tile([P, 2, 2, P], F32, name="tp", tag="tp", bufs=5)
             trs = []
             for s in (0, 1):
                 for u in (0, 1):
                     lo = 256 * (2 * h + s)
-                    trs.append((bank[:, s, u, :], words[:, lo + u : lo + 256 : 2]))
+                    if ordered is None:
+                        trs.append((bank[:, s, u, :], words[:, lo + u : lo + 256 : 2]))
+                    else:
+                        trs.append((bank[:, s, u, :], ordered[:, s, u, :]))
             dst = grouped[:].bitcast(F32)[:, 512 * h : 512 * (h + 1)].rearrange("p (s m u) -> p s m u", s=2, u=2)
             return trs, (dst, bank[:].rearrange("p s u m -> p s m u"))
 
@@ -91,13 +95,15 @@ def tile_cptensorproduct_pa_kernel(tc, x1, A, t2, w, C, out):
         t3_sb = {}
         w_rest = []
         quants = []
+        sorted_words = {}
 
         for i in range(-3, NB + 3):
             j = i + 2
             t3 = None
             if 0 <= i < NB:
                 t1_ps[i] = psum.tile([P, 4, CO], F32, name="t1", tag="t1", bufs=2)
-                t1_matmuls(i, (0, 1))
+                before = (0, 1) if i < NB - 1 else ()
+                t1_matmuls(i, before)
                 t3 = psum.tile([P, 4, CO], T3_DT, name="t3", tag="t3", bufs=1)
                 tcd, tsc = t2_q[i]
                 wc, ws = w_q[i // 2]
@@ -115,7 +121,7 @@ def tile_cptensorproduct_pa_kernel(tc, x1, A, t2, w, C, out):
                     )
             outs = []
             for k, (b0, n) in enumerate(GROUPS):
-                if b0 + n + 2 == i:
+                if max(b0 + n + 2, C_TICK + 2) == i:
                     o_ps = psum.tile([P, 2, n * CO], F32, name="o_ps", tag="tp", bufs=5)
                     hc, hs = h_q[k]
                     for e in (0, 1):
@@ -131,7 +137,7 @@ def tile_cptensorproduct_pa_kernel(tc, x1, A, t2, w, C, out):
                         )
                     outs.append((k, b0, n, o_ps))
             if 0 <= i < NB:
-                t1_matmuls(i, (2, 3))
+                t1_matmuls(i, (2, 3) if i < NB - 1 else (0, 1, 2, 3))
 
             trs = []
             copies = []
@@ -146,7 +152,7 @@ def tile_cptensorproduct_pa_kernel(tc, x1, A, t2, w, C, out):
                 tcd = work.tile([P, R], U32, name="tcd", tag="tcd", align_bytes=64)
                 tsc = work.tile([P, R], U8, name="tsc", tag="tsc", align_bytes=64)
                 for h in (0, 1):
-                    t, c = half(t2_sb[j][:].bitcast(F32), h, tg)
+                    t, c = half(t2_sb[j][:].bitcast(F32), h, tg, sorted_words.get((j, h)))
                     trs += t
                     copies.append(c)
                 done.append((tg, tcd, tsc))
@@ -201,6 +207,14 @@ def tile_cptensorproduct_pa_kernel(tc, x1, A, t2, w, C, out):
                     hs = work.tile([P, n * CO], U8, name="hs", tag="hs", align_bytes=64)
                     quantize(h_grouped[k], hc, hs)
                     h_q[k] = (hc, hs)
+
+            if SORT_FROM <= j + 1 < NB:
+                sw = work.tile([P, 2, 2, P], F32, name="sw", tag="sw")
+                nc.vector.tensor_copy(
+                    out=sw[:],
+                    in_=t2_sb[j + 1][:].bitcast(F32)[:, 512:1024].rearrange("p (s m u) -> p s u m", s=2, u=2),
+                )
+                sorted_words[(j + 1, 1)] = sw
 
             for k, b0, n, o_ps in outs:
                 dst = o_sb[k][:].rearrange("p b e c -> p e b c")

@@ -11,12 +11,24 @@ BF16 = mybir.dt.bfloat16
 U32 = mybir.dt.uint32
 U8 = mybir.dt.uint8
 FP8X4 = mybir.dt.float8_e4m3fn_x4
-T3_DT = BF16
 
 P = 128
 NPAIR = NB // 2
-C_TICK = 4
+LEAD = 3
+W_LEAD = 2
 SORT_FROM = 3
+C_STEP = 1
+TP_BUFS = 4
+T3_BUFS = 2
+OUT_ACT = 1
+A_STEP = 0
+X_LEAD = 1
+T2_SPLIT = 2
+APERM_STEP = -1
+TAIL_T1 = 1
+LAST_BEFORE = (0, 1)
+O_AFTER = 1
+POSTPONE = 1
 GROUPS = [(b, 2) for b in range(0, NB - 2, 2)] + [(NB - 2, 1), (NB - 1, 1)]
 
 
@@ -38,20 +50,32 @@ def tile_cptensorproduct_pa_kernel(tc, x1, A, t2, w, C, out):
         def load_w(k):
             nc.sync.dma_start(out=w_sb[k][:], in_=w[2 * k : 2 * k + 2].rearrange("b c k -> c b k"))
 
-        load_w(0)
-        for b in range(NB):
-            nc.sync.dma_start(out=t2_sb[b][:], in_=t2[b].rearrange("(m t) k -> m (t k)", t=4))
-            if b % 2 == 1 and (b + 1) // 2 < NPAIR:
-                load_w((b + 1) // 2)
-            if b == 1:
-                nc.sync.dma_start(out=a_raw[:], in_=A.rearrange("(p e) r -> p (e r)", e=2))
-            if b % 4 == 1:
-                g = b // 4
+        def load_t2(b):
+            for h in range(T2_SPLIT if b == 0 else 1):
+                n = 4 // (T2_SPLIT if b == 0 else 1)
                 nc.sync.dma_start(
-                    out=x1_sb[g][:], in_=x1[4 * g : 4 * g + 4].rearrange("b (p e) c -> p b (e c)", e=2)
+                    out=t2_sb[b][:, n * CV * h : n * CV * (h + 1)].rearrange("p (t k) -> p t k", t=n),
+                    in_=t2[b].rearrange("(m t) k -> m t k", t=4)[:, n * h : n * (h + 1), :],
                 )
-            if b == C_TICK + 2:
-                nc.sync.dma_start(out=c_raw[:], in_=C.rearrange("(p e) r -> p (e r)", e=2))
+
+        def load_x1(g):
+            nc.sync.dma_start(out=x1_sb[g][:], in_=x1[4 * g : 4 * g + 4].rearrange("b (p e) c -> p b (e c)", e=2))
+
+        def load_a():
+            nc.sync.dma_start(out=a_raw[:], in_=A.rearrange("(p e) r -> p (e r)", e=2))
+
+        def load_c():
+            nc.sync.dma_start(out=c_raw[:], in_=C.rearrange("(p e) r -> p (e r)", e=2))
+
+        loads = [(-LEAD - 1, 0, load_w, 0), (A_STEP, 0, load_a, None), (C_STEP, 3, load_c, None)]
+        loads += [(max(2 * k - W_LEAD, -LEAD - 1), 1, load_w, k) for k in range(1, NPAIR)]
+        loads += [(b - LEAD, 2, load_t2, b) for b in range(NB)]
+        loads += [(4 * g - X_LEAD if g else A_STEP, 1, load_x1, g) for g in range(NB // 4)]
+        for step, rank, call, arg in sorted(loads, key=lambda q: (q[0], q[1])):
+            if arg is None:
+                call()
+            else:
+                call(arg)
 
         ident = keep.tile([P, P], F32, name="ident", tag="ident")
         make_identity(nc, ident[:])
@@ -60,8 +84,8 @@ def tile_cptensorproduct_pa_kernel(tc, x1, A, t2, w, C, out):
         c_codes = keep.tile([P, D], U32, name="c_codes", tag="c_codes", align_bytes=64)
         c_scales = keep.tile([P, D], U8, name="c_scales", tag="c_scales", align_bytes=64)
 
-        def half(words, h, grouped, ordered=None):
-            bank = psum.tile([P, 2, 2, P], F32, name="tp", tag="tp", bufs=5)
+        def bank_of(words, h, grouped, ordered=None):
+            bank = psum.tile([P, 2, 2, P], F32, name="tp", tag="tp", bufs=TP_BUFS)
             trs = []
             for s in (0, 1):
                 for u in (0, 1):
@@ -69,7 +93,7 @@ def tile_cptensorproduct_pa_kernel(tc, x1, A, t2, w, C, out):
                     if ordered is None:
                         trs.append((bank[:, s, u, :], words[:, lo + u : lo + 256 : 2]))
                     else:
-                        trs.append((bank[:, s, u, :], ordered[:, s, u, :]))
+                        trs.append((bank[:, s, u, :], ordered[:, 2 * h + s, u, :]))
             dst = grouped[:].bitcast(F32)[:, 512 * h : 512 * (h + 1)].rearrange("p (s m u) -> p s m u", s=2, u=2)
             return trs, (dst, bank[:].rearrange("p s u m -> p s m u"))
 
@@ -93,18 +117,24 @@ def tile_cptensorproduct_pa_kernel(tc, x1, A, t2, w, C, out):
         h_q = {}
         t1_ps = {}
         t3_sb = {}
-        w_rest = []
         quants = []
         sorted_words = {}
+        first_o = C_STEP + 2
+        qh_step = {}
+        o_done = set()
+        postponed = []
 
-        for i in range(-3, NB + 3):
-            j = i + 2
+        for i in range(-LEAD - 1, NB + 4):
+            j = i + LEAD
             t3 = None
             if 0 <= i < NB:
-                t1_ps[i] = psum.tile([P, 4, CO], F32, name="t1", tag="t1", bufs=2)
-                before = (0, 1) if i < NB - 1 else ()
+                if i + LEAD < NB or not TAIL_T1:
+                    t1_ps[i] = psum.tile([P, 4, CO], F32, name="t1", tag="t1", bufs=2)
+                else:
+                    t1_ps[i] = psum.tile([P, 4, CO], F32, name="t1", tag="tp", bufs=TP_BUFS)
+                before = (0, 1) if i + LEAD < NB else LAST_BEFORE
                 t1_matmuls(i, before)
-                t3 = psum.tile([P, 4, CO], T3_DT, name="t3", tag="t3", bufs=1)
+                t3 = psum.tile([P, 4, CO], BF16, name="t3", tag="t3", bufs=T3_BUFS)
                 tcd, tsc = t2_q[i]
                 wc, ws = w_q[i // 2]
                 cols = slice(CO * (i % 2), CO * (i % 2 + 1))
@@ -121,8 +151,8 @@ def tile_cptensorproduct_pa_kernel(tc, x1, A, t2, w, C, out):
                     )
             outs = []
             for k, (b0, n) in enumerate(GROUPS):
-                if max(b0 + n + 2, C_TICK + 2) == i:
-                    o_ps = psum.tile([P, 2, n * CO], F32, name="o_ps", tag="tp", bufs=5)
+                if k in qh_step and k not in o_done and max(qh_step[k] + 1, first_o) <= i and (i != NB - 1 or not O_AFTER):
+                    o_ps = psum.tile([P, 2, n * CO], F32, name="o_ps", tag="tp", bufs=TP_BUFS)
                     hc, hs = h_q[k]
                     for e in (0, 1):
                         rows = slice(P * e, P * (e + 1))
@@ -136,43 +166,36 @@ def tile_cptensorproduct_pa_kernel(tc, x1, A, t2, w, C, out):
                             stop=True,
                         )
                     outs.append((k, b0, n, o_ps))
+                    o_done.add(k)
             if 0 <= i < NB:
-                t1_matmuls(i, (2, 3) if i < NB - 1 else (0, 1, 2, 3))
+                t1_matmuls(i, [t for t in range(4) if t not in before])
 
             trs = []
             copies = []
             done = []
-            for t, c, q in w_rest:
-                trs += t
-                copies.append(c)
-                done.append(q)
-            w_rest = []
+            if (i + W_LEAD) % 2 == 0 and 0 <= (i + W_LEAD) // 2 < NPAIR or i == -LEAD - 1:
+                k = max(0, (i + W_LEAD) // 2)
+                if k not in w_q:
+                    wg = work.tile([P, 4 * 2 * CO], BF16, name="wg", tag="wg", align_bytes=64)
+                    wc = work.tile([P, 2 * CO], U32, name="wc", tag="wc", bufs=4, align_bytes=64)
+                    ws = work.tile([P, 2 * CO], U8, name="ws", tag="ws", bufs=4, align_bytes=64)
+                    t, c = bank_of(w_sb[k][:].rearrange("p b k -> p (b k)").bitcast(F32), 0, wg)
+                    w_q[k] = (wc, ws)
+                    trs += t
+                    copies.append(c)
+                    done.append((wg, wc, ws))
             if 0 <= j < NB:
                 tg = work.tile([P, 4 * R], BF16, name="tg", tag="tg", align_bytes=64)
-                tcd = work.tile([P, R], U32, name="tcd", tag="tcd", align_bytes=64)
-                tsc = work.tile([P, R], U8, name="tsc", tag="tsc", align_bytes=64)
+                tcd = work.tile([P, R], U32, name="tcd", tag="tcd", bufs=LEAD + 2, align_bytes=64)
+                tsc = work.tile([P, R], U8, name="tsc", tag="tsc", bufs=LEAD + 2, align_bytes=64)
                 for h in (0, 1):
-                    t, c = half(t2_sb[j][:].bitcast(F32), h, tg, sorted_words.get((j, h)))
+                    t, c = bank_of(t2_sb[j][:].bitcast(F32), h, tg, sorted_words.get(j))
                     trs += t
                     copies.append(c)
                 done.append((tg, tcd, tsc))
                 t2_q[j] = (tcd, tsc)
-            if i % 2 == 1 and (i + 3) // 2 < NPAIR:
-                k = (i + 3) // 2
-                wg = work.tile([P, 4 * 2 * CO], BF16, name="wg", tag="wg", align_bytes=64)
-                wc = work.tile([P, 2 * CO], U32, name="wc", tag="wc", align_bytes=64)
-                ws = work.tile([P, 2 * CO], U8, name="ws", tag="ws", align_bytes=64)
-                t, c = half(w_sb[k][:].rearrange("p b k -> p (b k)").bitcast(F32), 0, wg)
-                w_q[k] = (wc, ws)
-                if k == 0:
-                    trs += t
-                    copies.append(c)
-                    done.append((wg, wc, ws))
-                else:
-                    trs += t[:2]
-                    w_rest.append((t[2:], c, (wg, wc, ws)))
-            if i == C_TICK:
-                t, c = half(c_raw[:].bitcast(F32), 0, c_grouped)
+            if i == C_STEP:
+                t, c = bank_of(c_raw[:].bitcast(F32), 0, c_grouped)
                 trs += t
                 copies.append(c)
                 done.append((c_grouped, c_codes, c_scales))
@@ -180,11 +203,19 @@ def tile_cptensorproduct_pa_kernel(tc, x1, A, t2, w, C, out):
                 nc.tensor.transpose(o, s, ident[:])
 
             if t3 is not None:
-                t3_sb[i] = work.tile([P, 4, CO], T3_DT, name="t3c", tag="t3c")
+                t3_sb[i] = work.tile([P, 4, CO], BF16, name="t3c", tag="t3c")
                 nc.scalar.copy(out=t3_sb[i][:], in_=t3[:])
+            for k, b0, n, o_ps in outs:
+                if OUT_ACT or i >= NB:
+                    nc.scalar.copy(
+                        out=o_sb[k][:].rearrange("p b e c -> p e b c"),
+                        in_=o_ps[:].rearrange("p e (b c) -> p e b c", b=n),
+                    )
             for dst, src in copies:
                 nc.scalar.copy(out=dst, in_=src)
 
+            if i == APERM_STEP:
+                nc.vector.tensor_copy(out=a_perm[:], in_=a_raw[:].rearrange("p (e m t) -> p e t m", e=2, t=4))
             for k, (b0, n) in enumerate(GROUPS):
                 if b0 == i - 1:
                     h_grouped[k] = work.tile([P, n * CO * 4], BF16, name="hg", tag="hg", align_bytes=64)
@@ -196,33 +227,38 @@ def tile_cptensorproduct_pa_kernel(tc, x1, A, t2, w, C, out):
                         in1=t3_sb[i - 1][:].rearrange("p t c -> p c t"),
                         op=mybir.AluOpType.mult,
                     )
+            between = len(quants) + len(postponed)
+            ready = postponed
+            postponed = []
             for grouped, codes, scales in quants:
                 quantize(grouped, codes, scales)
             quants = done
-            if i == -1:
-                nc.vector.tensor_copy(out=a_perm[:], in_=a_raw[:].rearrange("p (e m t) -> p e t m", e=2, t=4))
             for k, (b0, n) in enumerate(GROUPS):
-                if b0 + n + 1 == i:
-                    hc = work.tile([P, n * CO], U32, name="hc", tag="hc", align_bytes=64)
-                    hs = work.tile([P, n * CO], U8, name="hs", tag="hs", align_bytes=64)
-                    quantize(h_grouped[k], hc, hs)
-                    h_q[k] = (hc, hs)
-
+                if b0 + n == i:
+                    if between or not POSTPONE:
+                        ready.append(k)
+                    else:
+                        postponed.append(k)
+            for k in ready:
+                n = GROUPS[k][1]
+                hc = work.tile([P, n * CO], U32, name="hc", tag="hc", align_bytes=64)
+                hs = work.tile([P, n * CO], U8, name="hs", tag="hs", align_bytes=64)
+                quantize(h_grouped[k], hc, hs)
+                h_q[k] = (hc, hs)
+                qh_step[k] = i
             if SORT_FROM <= j + 1 < NB:
-                sw = work.tile([P, 2, 2, P], F32, name="sw", tag="sw")
+                sw = work.tile([P, 4, 2, P], F32, name="sw", tag="sw")
                 nc.vector.tensor_copy(
-                    out=sw[:],
-                    in_=t2_sb[j + 1][:].bitcast(F32)[:, 512:1024].rearrange("p (s m u) -> p s u m", s=2, u=2),
+                    out=sw[:], in_=t2_sb[j + 1][:].bitcast(F32).rearrange("p (s m u) -> p s u m", s=4, u=2)
                 )
-                sorted_words[(j + 1, 1)] = sw
+                sorted_words[j + 1] = sw
 
             for k, b0, n, o_ps in outs:
-                dst = o_sb[k][:].rearrange("p b e c -> p e b c")
-                src = o_ps[:].rearrange("p e (b c) -> p e b c", b=n)
-                if i < NB:
-                    nc.vector.tensor_copy(out=dst, in_=src)
-                else:
-                    nc.scalar.copy(out=dst, in_=src)
+                if not (OUT_ACT or i >= NB):
+                    nc.vector.tensor_copy(
+                        out=o_sb[k][:].rearrange("p b e c -> p e b c"),
+                        in_=o_ps[:].rearrange("p e (b c) -> p e b c", b=n),
+                    )
                 nc.sync.dma_start(
                     out=out[b0 : b0 + n].rearrange("b (p e) c -> p b (e c)", e=2),
                     in_=o_sb[k][:].rearrange("p b e c -> p b (e c)"),

@@ -29,6 +29,8 @@ TAIL_T1 = 1
 LAST_BEFORE = (0, 1)
 O_AFTER = 1
 POSTPONE = 1
+SORT_SLOTS = 3
+W_COPY_DVE = 0
 GROUPS = [(b, 2) for b in range(0, NB - 2, 2)] + [(NB - 2, 1), (NB - 1, 1)]
 
 
@@ -90,10 +92,10 @@ def tile_cptensorproduct_pa_kernel(tc, x1, A, t2, w, C, out):
             for s in (0, 1):
                 for u in (0, 1):
                     lo = 256 * (2 * h + s)
-                    if ordered is None:
+                    if ordered is None or 2 * h + s < 4 - SORT_SLOTS:
                         trs.append((bank[:, s, u, :], words[:, lo + u : lo + 256 : 2]))
                     else:
-                        trs.append((bank[:, s, u, :], ordered[:, 2 * h + s, u, :]))
+                        trs.append((bank[:, s, u, :], ordered[:, 2 * h + s - (4 - SORT_SLOTS), u, :]))
             dst = grouped[:].bitcast(F32)[:, 512 * h : 512 * (h + 1)].rearrange("p (s m u) -> p s m u", s=2, u=2)
             return trs, (dst, bank[:].rearrange("p s u m -> p s m u"))
 
@@ -172,6 +174,7 @@ def tile_cptensorproduct_pa_kernel(tc, x1, A, t2, w, C, out):
 
             trs = []
             copies = []
+            dve_copies = []
             done = []
             if (i + W_LEAD) % 2 == 0 and 0 <= (i + W_LEAD) // 2 < NPAIR or i == -LEAD - 1:
                 k = max(0, (i + W_LEAD) // 2)
@@ -182,7 +185,10 @@ def tile_cptensorproduct_pa_kernel(tc, x1, A, t2, w, C, out):
                     t, c = bank_of(w_sb[k][:].rearrange("p b k -> p (b k)").bitcast(F32), 0, wg)
                     w_q[k] = (wc, ws)
                     trs += t
-                    copies.append(c)
+                    if W_COPY_DVE:
+                        dve_copies.append(c)
+                    else:
+                        copies.append(c)
                     done.append((wg, wc, ws))
             if 0 <= j < NB:
                 tg = work.tile([P, 4 * R], BF16, name="tg", tag="tg", align_bytes=64)
@@ -246,10 +252,15 @@ def tile_cptensorproduct_pa_kernel(tc, x1, A, t2, w, C, out):
                 quantize(h_grouped[k], hc, hs)
                 h_q[k] = (hc, hs)
                 qh_step[k] = i
+            for dst, src in dve_copies:
+                nc.vector.tensor_copy(out=dst, in_=src)
             if SORT_FROM <= j + 1 < NB:
-                sw = work.tile([P, 4, 2, P], F32, name="sw", tag="sw")
+                sw = work.tile([P, SORT_SLOTS, 2, P], F32, name="sw", tag="sw")
                 nc.vector.tensor_copy(
-                    out=sw[:], in_=t2_sb[j + 1][:].bitcast(F32).rearrange("p (s m u) -> p s u m", s=4, u=2)
+                    out=sw[:].rearrange("p s u m -> p u s m"),
+                    in_=t2_sb[j + 1][:].bitcast(F32)[:, 256 * (4 - SORT_SLOTS) :].rearrange(
+                        "p (s m u) -> p u s m", s=SORT_SLOTS, u=2
+                    ),
                 )
                 sorted_words[j + 1] = sw
 

@@ -31,6 +31,8 @@ O_AFTER = 1
 POSTPONE = 1
 SORT_SLOTS = 3
 W_COPY_DVE = 0
+WARM_FIRST = 3
+WARM_EACH = 1
 GROUPS = [(b, 2) for b in range(0, NB - 2, 2)] + [(NB - 2, 1), (NB - 1, 1)]
 
 
@@ -98,6 +100,19 @@ def tile_cptensorproduct_pa_kernel(tc, x1, A, t2, w, C, out):
                         trs.append((bank[:, s, u, :], ordered[:, 2 * h + s - (4 - SORT_SLOTS), u, :]))
             dst = grouped[:].bitcast(F32)[:, 512 * h : 512 * (h + 1)].rearrange("p (s m u) -> p s m u", s=2, u=2)
             return trs, (dst, bank[:].rearrange("p s u m -> p s m u"))
+
+        warm_sb = keep.tile([P, 4 * P], BF16, name="warm_sb", tag="warm_sb")
+        if WARM_FIRST or WARM_EACH:
+            nc.vector.memset(warm_sb[:], 0.0)
+            warm_ps = psum.tile([P, 4, CO], F32, name="t1", tag="t1", bufs=2)
+
+        def warm(n):
+            for q in range(n):
+                nc.tensor.matmul(
+                    warm_ps[:].rearrange("p t c -> p (t c)"), lhsT=warm_sb[:, 0:P], rhs=warm_sb[:], start=True, stop=True
+                )
+
+        warm(WARM_FIRST)
 
         def quantize(grouped, codes, scales):
             nc.vector.quantize_mx(out=codes[:].bitcast(FP8X4), scales=scales[:], in_=grouped[:])
@@ -185,7 +200,7 @@ def tile_cptensorproduct_pa_kernel(tc, x1, A, t2, w, C, out):
                     t, c = bank_of(w_sb[k][:].rearrange("p b k -> p (b k)").bitcast(F32), 0, wg)
                     w_q[k] = (wc, ws)
                     trs += t
-                    if W_COPY_DVE:
+                    if W_COPY_DVE == 1 or (W_COPY_DVE == 2 and k % 2 == 1):
                         dve_copies.append(c)
                     else:
                         copies.append(c)
@@ -207,6 +222,8 @@ def tile_cptensorproduct_pa_kernel(tc, x1, A, t2, w, C, out):
                 done.append((c_grouped, c_codes, c_scales))
             for o, s in trs:
                 nc.tensor.transpose(o, s, ident[:])
+            if -LEAD <= i < 0:
+                warm(WARM_EACH)
 
             if t3 is not None:
                 t3_sb[i] = work.tile([P, 4, CO], BF16, name="t3c", tag="t3c")

@@ -29,7 +29,8 @@ TAIL_T1 = 1
 LAST_BEFORE = (0, 1)
 O_AFTER = 1
 POSTPONE = 1
-SORT_SLOTS = 3
+SORT_SLOTS = 4
+NEIGH = 4
 W_COPY_DVE = 0
 WARM_FIRST = 3
 WARM_EACH = 1
@@ -245,9 +246,9 @@ def tile_cptensorproduct_pa_kernel(tc, x1, A, t2, w, C, out):
                 if b0 <= i - 1 < b0 + n:
                     lo = 4 * CO * (i - 1 - b0)
                     nc.vector.tensor_tensor(
-                        out=h_grouped[k][:, lo : lo + 4 * CO].rearrange("p (c t) -> p c t", t=4),
-                        in0=t1_ps[i - 1][:].rearrange("p t c -> p c t"),
-                        in1=t3_sb[i - 1][:].rearrange("p t c -> p c t"),
+                        out=h_grouped[k][:, lo : lo + 4 * CO].rearrange("p (c n t) -> p c t n", n=NEIGH, t=4),
+                        in0=t1_ps[i - 1][:].rearrange("p t (c n) -> p c t n", n=NEIGH),
+                        in1=t3_sb[i - 1][:].rearrange("p t (c n) -> p c t n", n=NEIGH),
                         op=mybir.AluOpType.mult,
                     )
             between = len(quants) + len(postponed)

@@ -29,12 +29,17 @@ TAIL_T1 = 1
 LAST_BEFORE = (0, 1)
 O_AFTER = 1
 POSTPONE = 1
-SORT_SLOTS = 4
+SORT_SLOTS = 3
 NEIGH = 4
+FOUR = (3, 4, 5, 6, 7, 8, 9, 10, 11, 12, 13, 14, 15)
 W_COPY_DVE = 0
 WARM_FIRST = 3
 WARM_EACH = 1
 GROUPS = [(b, 2) for b in range(0, NB - 2, 2)] + [(NB - 2, 1), (NB - 1, 1)]
+
+
+def slots_of(b):
+    return 4 if b in FOUR else SORT_SLOTS
 
 
 def tile_cptensorproduct_pa_kernel(tc, x1, A, t2, w, C, out):
@@ -95,10 +100,10 @@ def tile_cptensorproduct_pa_kernel(tc, x1, A, t2, w, C, out):
             for s in (0, 1):
                 for u in (0, 1):
                     lo = 256 * (2 * h + s)
-                    if ordered is None or 2 * h + s < 4 - SORT_SLOTS:
+                    if ordered is None or 2 * h + s < 4 - ordered[1]:
                         trs.append((bank[:, s, u, :], words[:, lo + u : lo + 256 : 2]))
                     else:
-                        trs.append((bank[:, s, u, :], ordered[:, 2 * h + s - (4 - SORT_SLOTS), u, :]))
+                        trs.append((bank[:, s, u, :], ordered[0][:, u, 2 * h + s - (4 - ordered[1]), :]))
             dst = grouped[:].bitcast(F32)[:, 512 * h : 512 * (h + 1)].rearrange("p (s m u) -> p s m u", s=2, u=2)
             return trs, (dst, bank[:].rearrange("p s u m -> p s m u"))
 
@@ -273,14 +278,15 @@ def tile_cptensorproduct_pa_kernel(tc, x1, A, t2, w, C, out):
             for dst, src in dve_copies:
                 nc.vector.tensor_copy(out=dst, in_=src)
             if SORT_FROM <= j + 1 < NB:
-                sw = work.tile([P, SORT_SLOTS, 2, P], F32, name="sw", tag="sw")
+                ns = slots_of(j + 1)
+                sw = work.tile([P, 2, ns, P], F32, name="sw", tag="sw")
                 nc.vector.tensor_copy(
-                    out=sw[:].rearrange("p s u m -> p u s m"),
-                    in_=t2_sb[j + 1][:].bitcast(F32)[:, 256 * (4 - SORT_SLOTS) :].rearrange(
-                        "p (s m u) -> p u s m", s=SORT_SLOTS, u=2
+                    out=sw[:].rearrange("p u s (b n) -> p (s b) u n", n=4),
+                    in_=t2_sb[j + 1][:].bitcast(F32)[:, 256 * (4 - ns) :].rearrange(
+                        "p (s b n u) -> p (s b) u n", s=ns, n=4, u=2
                     ),
                 )
-                sorted_words[j + 1] = sw
+                sorted_words[j + 1] = (sw, ns)
 
             for k, b0, n, o_ps in outs:
                 if not (OUT_ACT or i >= NB):

@@ -31,7 +31,7 @@ O_AFTER = 1
 POSTPONE = 1
 SORT_SLOTS = 3
 NEIGH = 4
-FOUR = (3, 4, 5, 6, 7, 8, 9, 10, 11, 12, 13, 14, 15)
+FOUR = (4, 6, 8, 10, 12, 14)
 W_COPY_DVE = 0
 WARM_FIRST = 3
 WARM_EACH = 1

@@ -33,8 +33,6 @@ SORT_SLOTS = 3
 NEIGH = 4
 FOUR = (4, 6, 8, 10, 12, 14)
 W_COPY_DVE = 0
-WARM_FIRST = 3
-WARM_EACH = 1
 GROUPS = [(b, 2) for b in range(0, NB - 2, 2)] + [(NB - 2, 1), (NB - 1, 1)]
 
 
@@ -106,19 +104,6 @@ def tile_cptensorproduct_pa_kernel(tc, x1, A, t2, w, C, out):
                         trs.append((bank[:, s, u, :], ordered[0][:, u, 2 * h + s - (4 - ordered[1]), :]))
             dst = grouped[:].bitcast(F32)[:, 512 * h : 512 * (h + 1)].rearrange("p (s m u) -> p s m u", s=2, u=2)
             return trs, (dst, bank[:].rearrange("p s u m -> p s m u"))
-
-        warm_sb = keep.tile([P, 4 * P], BF16, name="warm_sb", tag="warm_sb")
-        if WARM_FIRST or WARM_EACH:
-            nc.vector.memset(warm_sb[:], 0.0)
-            warm_ps = psum.tile([P, 4, CO], F32, name="t1", tag="t1", bufs=2)
-
-        def warm(n):
-            for q in range(n):
-                nc.tensor.matmul(
-                    warm_ps[:].rearrange("p t c -> p (t c)"), lhsT=warm_sb[:, 0:P], rhs=warm_sb[:], start=True, stop=True
-                )
-
-        warm(WARM_FIRST)
 
         def quantize(grouped, codes, scales):
             nc.vector.quantize_mx(out=codes[:].bitcast(FP8X4), scales=scales[:], in_=grouped[:])
@@ -228,8 +213,6 @@ def tile_cptensorproduct_pa_kernel(tc, x1, A, t2, w, C, out):
                 done.append((c_grouped, c_codes, c_scales))
             for o, s in trs:
                 nc.tensor.transpose(o, s, ident[:])
-            if -LEAD <= i < 0:
-                warm(WARM_EACH)
 
             if t3 is not None:
                 t3_sb[i] = work.tile([P, 4, CO], BF16, name="t3c", tag="t3c")

from contextlib import ExitStack

import concourse.mybir as mybir
from concourse.masks import make_identity

NB, D, CO, CV, R = 16, 256, 128, 512, 512
FLOPS = 2 * NB * CO * (R * D + R * CV + D * R)

F32 = mybir.dt.float32
BF16 = mybir.dt.bfloat16
U32 = mybir.dt.uint32
U8 = mybir.dt.uint8
FP8X4 = mybir.dt.float8_e4m3fn_x4

P = 128
NPAIR = NB // 2
LEAD = 3
W_LEAD = 2
SORT_FROM = 3
C_STEP = 1
TP_BUFS = 4
T3_BUFS = 2
OUT_ACT = 1
A_STEP = 0
X_LEAD = 1
T2_SPLIT = 2
APERM_STEP = -1
TAIL_T1 = 1
LAST_BEFORE = (0, 1)
O_AFTER = 1
POSTPONE = 1
SORT_SLOTS = 3
NEIGH = 4
FOUR = (4, 6, 8, 10, 12, 14)
W_COPY_DVE = 0
GROUPS = [(b, 2) for b in range(0, NB - 2, 2)] + [(NB - 2, 1), (NB - 1, 1)]


def slots_of(b):
    return 4 if b in FOUR else SORT_SLOTS


def tile_cptensorproduct_pa_kernel(tc, x1, A, t2, w, C, out):
    nc = tc.nc
    with ExitStack() as ctx:
        keep = ctx.enter_context(tc.tile_pool(name="keep", bufs=1))
        work = ctx.enter_context(tc.tile_pool(name="work", bufs=3))
        psum = ctx.enter_context(tc.psum_pool(name="psum", bufs=1))
        ctx.enter_context(tc.manual_schedule())

        t2_sb = [keep.tile([P, 4 * CV], BF16, name="t2_sb%d" % b, tag="t2_sb%d" % b) for b in range(NB)]
        w_sb = [keep.tile([P, 2, CV], BF16, name="w_sb%d" % k, tag="w_sb%d" % k) for k in range(NPAIR)]
        x1_sb = [keep.tile([P, 4, 2 * CO], BF16, name="x1_sb%d" % g, tag="x1_sb%d" % g) for g in range(NB // 4)]
        o_sb = [keep.tile([P, n, 2, CO], F32, name="o_sb%d" % b, tag="o_sb%d" % b) for b, n in GROUPS]
        a_raw = keep.tile([P, 2 * R], BF16, name="a_raw", tag="a_raw")
        c_raw = keep.tile([P, 2 * R], BF16, name="c_raw", tag="c_raw")

        def load_w(k):
            nc.sync.dma_start(out=w_sb[k][:], in_=w[2 * k : 2 * k + 2].rearrange("b c k -> c b k"))

        def load_t2(b):
            for h in range(T2_SPLIT if b == 0 else 1):
                n = 4 // (T2_SPLIT if b == 0 else 1)
                nc.sync.dma_start(
                    out=t2_sb[b][:, n * CV * h : n * CV * (h + 1)].rearrange("p (t k) -> p t k", t=n),
                    in_=t2[b].rearrange("(m t) k -> m t k", t=4)[:, n * h : n * (h + 1), :],
                )

        def load_x1(g):
            nc.sync.dma_start(out=x1_sb[g][:], in_=x1[4 * g : 4 * g + 4].rearrange("b (p e) c -> p b (e c)", e=2))

        def load_a():
            nc.sync.dma_start(out=a_raw[:], in_=A.rearrange("(p e) r -> p (e r)", e=2))

        def load_c():
            nc.sync.dma_start(out=c_raw[:], in_=C.rearrange("(p e) r -> p (e r)", e=2))

        loads = [(-LEAD - 1, 0, load_w, 0), (A_STEP, 0, load_a, None), (C_STEP, 3, load_c, None)]
        loads += [(max(2 * k - W_LEAD, -LEAD - 1), 1, load_w, k) for k in range(1, NPAIR)]
        loads += [(b - LEAD, 2, load_t2, b) for b in range(NB)]
        loads += [(4 * g - X_LEAD if g else A_STEP, 1, load_x1, g) for g in range(NB // 4)]
        for step, rank, call, arg in sorted(loads, key=lambda q: (q[0], q[1])):
            if arg is None:
                call()
            else:
                call(arg)

        ident = keep.tile([P, P], F32, name="ident", tag="ident")
        make_identity(nc, ident[:])
        a_perm = keep.tile([P, 2, 4, P], BF16, name="a_perm", tag="a_perm")
        c_grouped = keep.tile([P, 4 * D], BF16, name="c_grouped", tag="c_grouped", align_bytes=64)
        c_codes = keep.tile([P, D], U32, name="c_codes", tag="c_codes", align_bytes=64)
        c_scales = keep.tile([P, D], U8, name="c_scales", tag="c_scales", align_bytes=64)

        def bank_of(words, h, grouped, ordered=None):
            bank = psum.tile([P, 2, 2, P], F32, name="tp", tag="tp", bufs=TP_BUFS)
            trs = []
            for s in (0, 1):
                for u in (0, 1):
                    lo = 256 * (2 * h + s)
                    if ordered is None or 2 * h + s < 4 - ordered[1]:
                        trs.append((bank[:, s, u, :], words[:, lo + u : lo + 256 : 2]))
                    else:
                        trs.append((bank[:, s, u, :], ordered[0][:, u, 2 * h + s - (4 - ordered[1]), :]))
            dst = grouped[:].bitcast(F32)[:, 512 * h : 512 * (h + 1)].rearrange("p (s m u) -> p s m u", s=2, u=2)
            return trs, (dst, bank[:].rearrange("p s u m -> p s m u"))

        def quantize(grouped, codes, scales):
            nc.vector.quantize_mx(out=codes[:].bitcast(FP8X4), scales=scales[:], in_=grouped[:])

        def t1_matmuls(b, slots):
            for t in slots:
                for e in (0, 1):
                    nc.tensor.matmul(
                        t1_ps[b][:, t, :],
                        lhsT=a_perm[:, e, t, :],
                        rhs=x1_sb[b // 4][:, b % 4, CO * e : CO * (e + 1)],
                        start=(e == 0),
                        stop=(e == 1),
                    )

        t2_q = {}
        w_q = {}
        h_grouped = {}
        h_q = {}
        t1_ps = {}
        t3_sb = {}
        quants = []
        sorted_words = {}
        first_o = C_STEP + 2
        qh_step = {}
        o_done = set()
        postponed = []

        for i in range(-LEAD - 1, NB + 4):
            j = i + LEAD
            t3 = None
            if 0 <= i < NB:
                if i + LEAD < NB or not TAIL_T1:
                    t1_ps[i] = psum.tile([P, 4, CO], F32, name="t1", tag="t1", bufs=2)
                else:
                    t1_ps[i] = psum.tile([P, 4, CO], F32, name="t1", tag="tp", bufs=TP_BUFS)
                before = (0, 1) if i + LEAD < NB else LAST_BEFORE
                t1_matmuls(i, before)
                t3 = psum.tile([P, 4, CO], BF16, name="t3", tag="t3", bufs=T3_BUFS)
                tcd, tsc = t2_q[i]
                wc, ws = w_q[i // 2]
                cols = slice(CO * (i % 2), CO * (i % 2 + 1))
                for t in range(4):
                    rows = slice(P * t, P * (t + 1))
                    nc.tensor.matmul_mx(
                        out=t3[:, t, :],
                        lhsT=tcd[:, rows].bitcast(FP8X4),
                        lhsT_scale=tsc[:, rows],
                        rhs=wc[:, cols].bitcast(FP8X4),
                        rhs_scale=ws[:, cols],
                        start=True,
                        stop=True,
                    )
            outs = []
            for k, (b0, n) in enumerate(GROUPS):
                if k in qh_step and k not in o_done and max(qh_step[k] + 1, first_o) <= i and (i != NB - 1 or not O_AFTER):
                    o_ps = psum.tile([P, 2, n * CO], F32, name="o_ps", tag="tp", bufs=TP_BUFS)
                    hc, hs = h_q[k]
                    for e in (0, 1):
                        rows = slice(P * e, P * (e + 1))
                        nc.tensor.matmul_mx(
                            out=o_ps[:, e, :],
                            lhsT=c_codes[:, rows].bitcast(FP8X4),
                            lhsT_scale=c_scales[:, rows],
                            rhs=hc[:].bitcast(FP8X4),
                            rhs_scale=hs[:],
                            start=True,
                            stop=True,
                        )
                    outs.append((k, b0, n, o_ps))
                    o_done.add(k)
            if 0 <= i < NB:
                t1_matmuls(i, [t for t in range(4) if t not in before])

            trs = []
            copies = []
            dve_copies = []
            done = []
            if (i + W_LEAD) % 2 == 0 and 0 <= (i + W_LEAD) // 2 < NPAIR or i == -LEAD - 1:
                k = max(0, (i + W_LEAD) // 2)
                if k not in w_q:
                    wg = work.tile([P, 4 * 2 * CO], BF16, name="wg", tag="wg", align_bytes=64)
                    wc = work.tile([P, 2 * CO], U32, name="wc", tag="wc", bufs=4, align_bytes=64)
                    ws = work.tile([P, 2 * CO], U8, name="ws", tag="ws", bufs=4, align_bytes=64)
                    t, c = bank_of(w_sb[k][:].rearrange("p b k -> p (b k)").bitcast(F32), 0, wg)
                    w_q[k] = (wc, ws)
                    trs += t
                    if W_COPY_DVE == 1 or (W_COPY_DVE == 2 and k % 2 == 1):
                        dve_copies.append(c)
                    else:
                        copies.append(c)
                    done.append((wg, wc, ws))
            if 0 <= j < NB:
                tg = work.tile([P, 4 * R], BF16, name="tg", tag="tg", align_bytes=64)
                tcd = work.tile([P, R], U32, name="tcd", tag="tcd", bufs=LEAD + 2, align_bytes=64)
                tsc = work.tile([P, R], U8, name="tsc", tag="tsc", bufs=LEAD + 2, align_bytes=64)
                for h in (0, 1):
                    t, c = bank_of(t2_sb[j][:].bitcast(F32), h, tg, sorted_words.get(j))
                    trs += t
                    copies.append(c)
                done.append((tg, tcd, tsc))
                t2_q[j] = (tcd, tsc)
            if i == C_STEP:
                t, c = bank_of(c_raw[:].bitcast(F32), 0, c_grouped)
                trs += t
                copies.append(c)
                done.append((c_grouped, c_codes, c_scales))
            for o, s in trs:
                nc.tensor.transpose(o, s, ident[:])

            if t3 is not None:
                t3_sb[i] = work.tile([P, 4, CO], BF16, name="t3c", tag="t3c")
                nc.scalar.copy(out=t3_sb[i][:], in_=t3[:])
            for k, b0, n, o_ps in outs:
                if OUT_ACT or i >= NB:
                    nc.scalar.copy(
                        out=o_sb[k][:].rearrange("p b e c -> p e b c"),
                        in_=o_ps[:].rearrange("p e (b c) -> p e b c", b=n),
                    )
            for dst, src in copies:
                nc.scalar.copy(out=dst, in_=src)

            if i == APERM_STEP:
                nc.vector.tensor_copy(out=a_perm[:], in_=a_raw[:].rearrange("p (e m t) -> p e t m", e=2, t=4))
            for k, (b0, n) in enumerate(GROUPS):
                if b0 == i - 1:
                    h_grouped[k] = work.tile([P, n * CO * 4], BF16, name="hg", tag="hg", align_bytes=64)
                if b0 <= i - 1 < b0 + n:
                    lo = 4 * CO * (i - 1 - b0)
                    nc.vector.tensor_tensor(
                        out=h_grouped[k][:, lo : lo + 4 * CO].rearrange("p (c n t) -> p c t n", n=NEIGH, t=4),
                        in0=t1_ps[i - 1][:].rearrange("p t (c n) -> p c t n", n=NEIGH),
                        in1=t3_sb[i - 1][:].rearrange("p t (c n) -> p c t n", n=NEIGH),
                        op=mybir.AluOpType.mult,
                    )
            between = len(quants) + len(postponed)
            ready = postponed
            postponed = []
            for grouped, codes, scales in quants:
                quantize(grouped, codes, scales)
            quants = done
            for k, (b0, n) in enumerate(GROUPS):
                if b0 + n == i:
                    if between or not POSTPONE:
                        ready.append(k)
                    else:
                        postponed.append(k)
            for k in ready:
                n = GROUPS[k][1]
                hc = work.tile([P, n * CO], U32, name="hc", tag="hc", align_bytes=64)
                hs = work.tile([P, n * CO], U8, name="hs", tag="hs", align_bytes=64)
                quantize(h_grouped[k], hc, hs)
                h_q[k] = (hc, hs)
                qh_step[k] = i
            for dst, src in dve_copies:
                nc.vector.tensor_copy(out=dst, in_=src)
            if SORT_FROM <= j + 1 < NB:
                ns = slots_of(j + 1)
                sw = work.tile([P, 2, ns, P], F32, name="sw", tag="sw")
                nc.vector.tensor_copy(
                    out=sw[:].rearrange("p u s (b n) -> p (s b) u n", n=4),
                    in_=t2_sb[j + 1][:].bitcast(F32)[:, 256 * (4 - ns) :].rearrange(
                        "p (s b n u) -> p (s b) u n", s=ns, n=4, u=2
                    ),
                )
                sorted_words[j + 1] = (sw, ns)

            for k, b0, n, o_ps in outs:
                if not (OUT_ACT or i >= NB):
                    nc.vector.tensor_copy(
                        out=o_sb[k][:].rearrange("p b e c -> p e b c"),
                        in_=o_ps[:].rearrange("p e (b c) -> p e b c", b=n),
                    )
                nc.sync.dma_start(
                    out=out[b0 : b0 + n].rearrange("b (p e) c -> p b (e c)", e=2),
                    in_=o_sb[k][:].rearrange("p b e c -> p b (e c)"),
                )
